import numpy as np
import ml_dtypes


def mxq(x, axis, fmt="e4m3"):
    dtype, down = {"e4m3": (ml_dtypes.float8_e4m3fn, 7), "e5m2": (ml_dtypes.float8_e5m2, 14)}[fmt]
    v = np.moveaxis(np.asarray(x, np.float32).astype(ml_dtypes.bfloat16).astype(np.float64), axis, -1)
    blocks = v.reshape(v.shape[:-1] + (-1, 32))
    amax = np.abs(blocks).max(-1, keepdims=True)
    byte = np.maximum(np.where(amax > 0, np.frexp(amax)[1] - 1 + 127, 0) - down, 1)
    scale = np.exp2(byte - 127.0)
    codes = (blocks / scale).astype(np.float32).astype(dtype).astype(np.float64)
    return np.moveaxis((codes * scale).reshape(v.shape), -1, axis)


WIDE = False


def mx_kscale(k):
    if not WIDE:
        return np.ones(k)
    levels = np.array([10, -10, 5, -5, 0])
    a = np.random.permutation(np.resize(levels, k // 512 * 4)).reshape(k // 512, 4)
    idx = np.arange(k)
    return np.exp2(a[idx // 512, idx % 128 // 32])


BF16 = ml_dtypes.bfloat16


def bf(x):
    return np.asarray(x, np.float32).astype(BF16)


def f64(x):
    return np.asarray(x).astype(np.float64)


N, MUL, RANK, D0, D1, D2 = 1024, 512, 128, 1, 3, 5
DIMS = (D0, D1, D2)
SD = D0 + D1 + D2
NI = len(DIMS)
SCALING = 2.0


def setup_inputs():
    s = mx_kscale(MUL)
    return {"x": bf(np.random.standard_normal((N, SD * MUL)) * np.tile(s, SD)),
            "a_lora": bf(np.random.standard_normal((N, SD * RANK)) * 0.5),
            "w_base": bf(np.random.standard_normal((NI, MUL, MUL)) / s[None, :, None]),
            "w_lora_b": bf(np.random.standard_normal((NI, RANK, MUL)))}


def reference(x, a_lora, w_base, w_lora_b):
    x, a_lora, w_base, w_lora_b = f64(x), f64(a_lora), f64(w_base), f64(w_lora_b)
    pw_base = 1.0 / np.sqrt(MUL)
    pw_b = 1.0 / np.sqrt(RANK)
    n = x.shape[0]
    outs = []
    off = 0
    offa = 0
    for k, d in enumerate(DIMS):
        seg = x[:, off:off + d * MUL].reshape(n * d, MUL)
        y = pw_base * (mxq(seg, 1, "e4m3") @ mxq(w_base[k], 0, "e4m3"))
        a = a_lora[:, offa:offa + d * RANK].reshape(n * d, RANK)
        b = pw_b * (a @ w_lora_b[k])
        outs.append((y + SCALING * b).reshape(n, d * MUL))
        off += d * MUL
        offa += d * RANK
    return np.concatenate(outs, axis=-1)

@@ -1,0 +1,215 @@
+import math
+from contextlib import ExitStack
+
+import concourse.mybir as mybir
+from concourse.masks import make_identity
+
+F32 = mybir.dt.float32
+BF16 = mybir.dt.bfloat16
+U32 = mybir.dt.uint32
+U8 = mybir.dt.uint8
+FP8X4 = mybir.dt.float8_e4m3fn_x4
+MULT = mybir.AluOpType.mult
+ADD = mybir.AluOpType.add
+
+P = 128
+PACK = 4
+NODES = 1024
+MUL = 512
+RANK = 128
+IRREP_OF_BLOCK = (0, 1, 1, 1, 2, 2, 2, 2, 2)
+BLOCKS = len(IRREP_OF_BLOCK)
+IRREPS = 3
+FIRST_USE = {
+    BLOCKS - 1 - j: IRREP_OF_BLOCK[j]
+    for j in range(BLOCKS)
+    if j == BLOCKS - 1 or IRREP_OF_BLOCK[j + 1] != IRREP_OF_BLOCK[j]
+}
+ROW_TILES = NODES // P
+PAIR = 2
+PAIRS = ROW_TILES // PAIR
+STEPS = PAIRS * BLOCKS
+HALVES = 2
+GROUP = 3
+LOOKAHEAD = 2
+STAGE_BUFS = 6
+
+BASE_FACTOR = 1.0 / math.sqrt(MUL)
+LORA_FACTOR = 2.0 / math.sqrt(RANK)
+
+FLOPS = 2 * NODES * BLOCKS * MUL * (MUL + RANK)
+
+
+def tile_loracuetlinear_pa_t_kernel(tc, x, a_lora, w_base, w_lora_b, out):
+    nc = tc.nc
+    x_rows = x.rearrange("(p r) c -> p r c", r=ROW_TILES)
+    a_rows = a_lora.rearrange("(p r) c -> p r c", r=ROW_TILES)
+    out_rows = out.rearrange("(p r) c -> p r c", r=ROW_TILES)
+
+    with ExitStack() as ctx:
+        keep = ctx.enter_context(tc.tile_pool(name="keep", bufs=1))
+        w_work = ctx.enter_context(tc.tile_pool(name="w_work", bufs=2))
+        x_work = ctx.enter_context(tc.tile_pool(name="x_work", bufs=3))
+        ready = ctx.enter_context(tc.tile_pool(name="ready", bufs=LOOKAHEAD + 2))
+        stages = ctx.enter_context(tc.tile_pool(name="stages", bufs=STAGE_BUFS))
+        psum = ctx.enter_context(tc.psum_pool(name="psum", bufs=2))
+        ctx.enter_context(tc.manual_schedule())
+
+        def pieces(pair):
+            return BLOCKS // GROUP if pair == 0 else 1
+
+        def row_tiles(name, width):
+            return [
+                [
+                    keep.tile([P, PAIR * (BLOCKS // pieces(pair)) * width], BF16, name="%s%d%d" % (name, pair, piece))
+                    for piece in range(pieces(pair))
+                ]
+                for pair in range(PAIRS)
+            ]
+
+        x_sb = row_tiles("x_sb", MUL)
+        a_sb = row_tiles("a_sb", RANK)
+        w_raw = [keep.tile([P, PACK * MUL], BF16, name="w_raw%d" % k) for k in range(IRREPS)]
+        w_codes = [keep.tile([P, MUL], U32, name="w_codes%d" % k, align_bytes=64) for k in range(IRREPS)]
+        w_scales = [keep.tile([P, MUL], U8, name="w_scales%d" % k, align_bytes=64) for k in range(IRREPS)]
+        wb_sb = [keep.tile([P, MUL], BF16, name="wb_sb%d" % k) for k in range(IRREPS)]
+        ident_f32 = keep.tile([P, P], F32, name="ident_f32")
+        ident_bf16 = keep.tile([P, P], BF16, name="ident_bf16")
+
+        def place(step):
+            pair, position = divmod(step, BLOCKS)
+            return pair, BLOCKS - 1 - position
+
+        def load_rows(pair, piece):
+            rows = slice(PAIR * pair, PAIR * (pair + 1))
+            blocks = BLOCKS // pieces(pair)
+            for sb, dram, width in ((x_sb, x_rows, MUL), (a_sb, a_rows, RANK)):
+                cols = slice(piece * blocks * width, (piece + 1) * blocks * width)
+                nc.sync.dma_start(
+                    out=sb[pair][piece][:].rearrange("p (i c) -> p i c", i=PAIR), in_=dram[:, rows, cols]
+                )
+
+        def block_of(sb, pair, i, j, width):
+            blocks = BLOCKS // pieces(pair)
+            return sb[pair][j // blocks], (i * blocks + j % blocks) * width
+
+        def load_weights(k):
+            nc.sync.dma_start(
+                out=w_raw[k][:].rearrange("q (u ec) -> q u ec", u=HALVES),
+                in_=w_base[k, :, :].rearrange("(u q e) c -> q u (e c)", u=HALVES, e=2),
+            )
+            nc.sync.dma_start(out=wb_sb[k][:], in_=w_lora_b[k, :, :])
+
+        def quantise_weights(k):
+            w_grouped = w_work.tile([P, MUL, PACK], BF16, name="w_grouped", align_bytes=64)
+            nc.vector.tensor_copy(out=w_grouped[:], in_=w_raw[k][:].rearrange("q (t c) -> q c t", t=PACK))
+            nc.vector.quantize_mx(
+                out=w_codes[k][:].bitcast(FP8X4),
+                scales=w_scales[k][:],
+                in_=w_grouped[:].rearrange("q c t -> q (c t)"),
+            )
+
+        def transpose_row_tile(step, i, xt, at):
+            pair, j = place(step)
+            x_tile, first = block_of(x_sb, pair, i, j, MUL)
+            for u in range(HALVES):
+                word = first // 2 + u * P
+                nc.tensor.transpose(xt[:, i, u, :], x_tile[:].bitcast(F32)[:, word : word + P], ident_f32[:])
+            a_tile, first = block_of(a_sb, pair, i, j, RANK)
+            nc.tensor.transpose(at[:, i, :], a_tile[:, first : first + RANK], ident_bf16[:])
+
+        load_weights(2)
+        load_rows(0, 2)
+        load_rows(0, 1)
+        load_weights(1)
+        load_rows(0, 0)
+        load_weights(0)
+        for pair in range(1, PAIRS):
+            load_rows(pair, 0)
+
+        make_identity(nc, ident_f32[:])
+        make_identity(nc, ident_bf16[:])
+
+        a_t = {}
+        x_codes = {}
+        x_scales = {}
+        stage = None
+
+        for step in range(-LOOKAHEAD, STEPS):
+            ahead = step + LOOKAHEAD
+            multiply = step >= 0
+            prepare = ahead < STEPS
+            if multiply:
+                pair, j = place(step)
+                k = IRREP_OF_BLOCK[j]
+                together = 1 if step >= STEPS - GROUP else GROUP
+                if j % together == together - 1:
+                    stage = stages.tile([P, PAIR, together * MUL], F32, name="stage")
+                cols = slice((j % together) * MUL, (j % together + 1) * MUL)
+            if prepare:
+                xt = psum.tile([P, PAIR, HALVES, P], F32, name="xt")
+                at = psum.tile([P, PAIR, P], BF16, name="at")
+
+            lora = []
+            for i in range(PAIR):
+                if multiply:
+                    lora_ps = psum.tile([P, MUL], F32, name="lora_ps")
+                    nc.tensor.matmul(
+                        lora_ps[:], lhsT=a_t[step][:, i, :], rhs=wb_sb[k][:], start=True, stop=True
+                    )
+                    lora.append(lora_ps)
+                if prepare:
+                    transpose_row_tile(ahead, i, xt, at)
+
+            if multiply:
+                for i in range(PAIR):
+                    nc.scalar.mul(out=stage[:, i, cols], in_=lora[i][:], mul=LORA_FACTOR)
+            if prepare:
+                x_grouped = x_work.tile([P, PAIR * P * PACK], BF16, name="x_grouped", align_bytes=64)
+                nc.scalar.copy(
+                    out=x_grouped[:].bitcast(F32).rearrange("q (i n u) -> q i n u", i=PAIR, u=HALVES),
+                    in_=xt[:].rearrange("q i u n -> q i n u"),
+                )
+
+            base = []
+            if multiply:
+                for i in range(PAIR):
+                    nodes = slice(i * P, (i + 1) * P)
+                    base_ps = psum.tile([P, MUL], F32, name="base_ps")
+                    nc.tensor.matmul_mx(
+                        out=base_ps[:],
+                        lhsT=x_codes[step][:, nodes].bitcast(FP8X4),
+                        lhsT_scale=x_scales[step][:, nodes],
+                        rhs=w_codes[k][:].bitcast(FP8X4),
+                        rhs_scale=w_scales[k][:],
+                        start=True,
+                        stop=True,
+                    )
+                    base.append(base_ps)
+
+            def finish(i):
+                nc.vector.scalar_tensor_tensor(
+                    out=stage[:, i, cols], in0=base[i][:], scalar=BASE_FACTOR, in1=stage[:, i, cols],
+                    op0=MULT, op1=ADD,
+                )
+
+            if ahead in FIRST_USE:
+                quantise_weights(FIRST_USE[ahead])
+            if multiply:
+                finish(0)
+            if prepare:
+                a_t[ahead] = ready.tile([P, PAIR, P], BF16, name="a_t")
+                nc.vector.tensor_copy(out=a_t[ahead][:], in_=at[:])
+            if multiply:
+                finish(1)
+            if prepare:
+                x_codes[ahead] = ready.tile([P, PAIR * P], U32, name="x_codes", align_bytes=64)
+                x_scales[ahead] = ready.tile([P, PAIR * P], U8, name="x_scales", align_bytes=64)
+                nc.vector.quantize_mx(
+                    out=x_codes[ahead][:].bitcast(FP8X4), scales=x_scales[ahead][:], in_=x_grouped[:]
+                )
+
+            if multiply and j % together == 0:
+                nc.sync.dma_start(
+                    out=out_rows[:, PAIR * pair : PAIR * (pair + 1), j * MUL : (j + together) * MUL], in_=stage[:]
+                )

@@ -170,6 +170,8 @@ def tile_loracuetlinear_pa_t_kernel(tc, x, a_lora, w_base, w_lora_b, out):
                     out=x_grouped[:].bitcast(F32).rearrange("q (i n u) -> q i n u", i=PAIR, u=HALVES),
                     in_=xt[:].rearrange("q i u n -> q i n u"),
                 )
+                a_t[ahead] = ready.tile([P, PAIR, P], BF16, name="a_t")
+                nc.scalar.copy(out=a_t[ahead][:], in_=at[:])
 
             base = []
             if multiply:
@@ -197,10 +199,6 @@ def tile_loracuetlinear_pa_t_kernel(tc, x, a_lora, w_base, w_lora_b, out):
                 quantise_weights(FIRST_USE[ahead])
             if multiply:
                 finish(0)
-            if prepare:
-                a_t[ahead] = ready.tile([P, PAIR, P], BF16, name="a_t")
-                nc.vector.tensor_copy(out=a_t[ahead][:], in_=at[:])
-            if multiply:
                 finish(1)
             if prepare:
                 x_codes[ahead] = ready.tile([P, PAIR * P], U32, name="x_codes", align_bytes=64)

@@ -32,6 +32,7 @@ STEPS = PAIRS * BLOCKS
 HALVES = 2
 GROUP = 3
 LOOKAHEAD = 2
+WEIGHT_LEAD = 5
 STAGE_BUFS = 6
 
 BASE_FACTOR = 1.0 / math.sqrt(MUL)
@@ -51,8 +52,12 @@ def tile_loracuetlinear_pa_t_kernel(tc, x, a_lora, w_base, w_lora_b, out):
         w_work = ctx.enter_context(tc.tile_pool(name="w_work", bufs=2))
         x_work = ctx.enter_context(tc.tile_pool(name="x_work", bufs=3))
         ready = ctx.enter_context(tc.tile_pool(name="ready", bufs=LOOKAHEAD + 2))
+        a_ready = ctx.enter_context(tc.tile_pool(name="a_ready", bufs=3))
         stages = ctx.enter_context(tc.tile_pool(name="stages", bufs=STAGE_BUFS))
-        psum = ctx.enter_context(tc.psum_pool(name="psum", bufs=2))
+        xt_banks = ctx.enter_context(tc.psum_pool(name="xt_banks", bufs=2))
+        at_banks = ctx.enter_context(tc.psum_pool(name="at_banks", bufs=1))
+        lora_banks = ctx.enter_context(tc.psum_pool(name="lora_banks", bufs=2))
+        base_banks = ctx.enter_context(tc.psum_pool(name="base_banks", bufs=3))
         ctx.enter_context(tc.manual_schedule())
 
         def pieces(pair):
@@ -102,7 +107,10 @@ def tile_loracuetlinear_pa_t_kernel(tc, x, a_lora, w_base, w_lora_b, out):
 
         def quantise_weights(k):
             w_grouped = w_work.tile([P, MUL, PACK], BF16, name="w_grouped", align_bytes=64)
-            nc.vector.tensor_copy(out=w_grouped[:], in_=w_raw[k][:].rearrange("q (t c) -> q c t", t=PACK))
+            nc.vector.tensor_copy(
+                out=w_grouped[:].rearrange("q (c r) t -> q c t r", r=4),
+                in_=w_raw[k][:].rearrange("q (t c r) -> q c t r", t=PACK, r=4),
+            )
             nc.vector.quantize_mx(
                 out=w_codes[k][:].bitcast(FP8X4),
                 scales=w_scales[k][:],
@@ -115,15 +123,17 @@ def tile_loracuetlinear_pa_t_kernel(tc, x, a_lora, w_base, w_lora_b, out):
             for u in range(HALVES):
                 word = first // 2 + u * P
                 nc.tensor.transpose(xt[:, i, u, :], x_tile[:].bitcast(F32)[:, word : word + P], ident_f32[:])
-            a_tile, first = block_of(a_sb, pair, i, j, RANK)
-            nc.tensor.transpose(at[:, i, :], a_tile[:, first : first + RANK], ident_bf16[:])
+            if step % GROUP == 0:
+                for later in range(GROUP):
+                    a_tile, first = block_of(a_sb, pair, i, j - later, RANK)
+                    nc.tensor.transpose(at[:, later, i, :], a_tile[:, first : first + RANK], ident_bf16[:])
 
         load_weights(2)
         load_rows(0, 2)
-        load_rows(0, 1)
         load_weights(1)
-        load_rows(0, 0)
+        load_rows(0, 1)
         load_weights(0)
+        load_rows(0, 0)
         for pair in range(1, PAIRS):
             load_rows(pair, 0)
 
@@ -135,10 +145,12 @@ def tile_loracuetlinear_pa_t_kernel(tc, x, a_lora, w_base, w_lora_b, out):
         x_scales = {}
         stage = None
 
-        for step in range(-LOOKAHEAD, STEPS):
+        at = None
+        for step in range(-WEIGHT_LEAD, STEPS):
             ahead = step + LOOKAHEAD
             multiply = step >= 0
-            prepare = ahead < STEPS
+            prepare = 0 <= ahead < STEPS
+            new_group = prepare and ahead % GROUP == 0
             if multiply:
                 pair, j = place(step)
                 k = IRREP_OF_BLOCK[j]
@@ -147,15 +159,20 @@ def tile_loracuetlinear_pa_t_kernel(tc, x, a_lora, w_base, w_lora_b, out):
                     stage = stages.tile([P, PAIR, together * MUL], F32, name="stage")
                 cols = slice((j % together) * MUL, (j % together + 1) * MUL)
             if prepare:
-                xt = psum.tile([P, PAIR, HALVES, P], F32, name="xt")
-                at = psum.tile([P, PAIR, P], BF16, name="at")
+                xt = xt_banks.tile([P, PAIR, HALVES, P], F32, name="xt")
+            if new_group:
+                at = at_banks.tile([P, GROUP, PAIR, P], BF16, name="at")
 
             lora = []
             for i in range(PAIR):
                 if multiply:
-                    lora_ps = psum.tile([P, MUL], F32, name="lora_ps")
+                    lora_ps = lora_banks.tile([P, MUL], F32, name="lora_ps")
                     nc.tensor.matmul(
-                        lora_ps[:], lhsT=a_t[step][:, i, :], rhs=wb_sb[k][:], start=True, stop=True
+                        lora_ps[:],
+                        lhsT=a_t[step // GROUP][:, step % GROUP, i, :],
+                        rhs=wb_sb[k][:],
+                        start=True,
+                        stop=True,
                     )
                     lora.append(lora_ps)
                 if prepare:
@@ -170,14 +187,12 @@ def tile_loracuetlinear_pa_t_kernel(tc, x, a_lora, w_base, w_lora_b, out):
                     out=x_grouped[:].bitcast(F32).rearrange("q (i n u) -> q i n u", i=PAIR, u=HALVES),
                     in_=xt[:].rearrange("q i u n -> q i n u"),
                 )
-                a_t[ahead] = ready.tile([P, PAIR, P], BF16, name="a_t")
-                nc.scalar.copy(out=a_t[ahead][:], in_=at[:])
 
             base = []
             if multiply:
                 for i in range(PAIR):
                     nodes = slice(i * P, (i + 1) * P)
-                    base_ps = psum.tile([P, MUL], F32, name="base_ps")
+                    base_ps = base_banks.tile([P, MUL], F32, name="base_ps")
                     nc.tensor.matmul_mx(
                         out=base_ps[:],
                         lhsT=x_codes[step][:, nodes].bitcast(FP8X4),
@@ -195,10 +210,14 @@ def tile_loracuetlinear_pa_t_kernel(tc, x, a_lora, w_base, w_lora_b, out):
                     op0=MULT, op1=ADD,
                 )
 
-            if ahead in FIRST_USE:
-                quantise_weights(FIRST_USE[ahead])
+            if step + WEIGHT_LEAD in FIRST_USE:
+                quantise_weights(FIRST_USE[step + WEIGHT_LEAD])
             if multiply:
                 finish(0)
+            if new_group:
+                a_t[ahead // GROUP] = a_ready.tile([P, GROUP, PAIR, P], BF16, name="a_t")
+                nc.vector.tensor_copy(out=a_t[ahead // GROUP][:], in_=at[:])
+            if multiply:
                 finish(1)
             if prepare:
                 x_codes[ahead] = ready.tile([P, PAIR * P], U32, name="x_codes", align_bytes=64)

import math
from contextlib import ExitStack

import concourse.mybir as mybir
from concourse.masks import make_identity

F32 = mybir.dt.float32
BF16 = mybir.dt.bfloat16
U32 = mybir.dt.uint32
U8 = mybir.dt.uint8
FP8X4 = mybir.dt.float8_e4m3fn_x4
MULT = mybir.AluOpType.mult
ADD = mybir.AluOpType.add

P = 128
PACK = 4
NODES = 1024
MUL = 512
RANK = 128
IRREP_OF_BLOCK = (0, 1, 1, 1, 2, 2, 2, 2, 2)
BLOCKS = len(IRREP_OF_BLOCK)
IRREPS = 3
FIRST_USE = {
    BLOCKS - 1 - j: IRREP_OF_BLOCK[j]
    for j in range(BLOCKS)
    if j == BLOCKS - 1 or IRREP_OF_BLOCK[j + 1] != IRREP_OF_BLOCK[j]
}
ROW_TILES = NODES // P
PAIR = 2
PAIRS = ROW_TILES // PAIR
STEPS = PAIRS * BLOCKS
HALVES = 2
GROUP = 3
LOOKAHEAD = 2
WEIGHT_LEAD = 5
STAGE_BUFS = 6

BASE_FACTOR = 1.0 / math.sqrt(MUL)
LORA_FACTOR = 2.0 / math.sqrt(RANK)

FLOPS = 2 * NODES * BLOCKS * MUL * (MUL + RANK)


def tile_loracuetlinear_pa_t_kernel(tc, x, a_lora, w_base, w_lora_b, out):
    nc = tc.nc
    x_rows = x.rearrange("(p r) c -> p r c", r=ROW_TILES)
    a_rows = a_lora.rearrange("(p r) c -> p r c", r=ROW_TILES)
    out_rows = out.rearrange("(p r) c -> p r c", r=ROW_TILES)

    with ExitStack() as ctx:
        keep = ctx.enter_context(tc.tile_pool(name="keep", bufs=1))
        w_work = ctx.enter_context(tc.tile_pool(name="w_work", bufs=2))
        x_work = ctx.enter_context(tc.tile_pool(name="x_work", bufs=3))
        ready = ctx.enter_context(tc.tile_pool(name="ready", bufs=LOOKAHEAD + 2))
        a_ready = ctx.enter_context(tc.tile_pool(name="a_ready", bufs=3))
        stages = ctx.enter_context(tc.tile_pool(name="stages", bufs=STAGE_BUFS))
        xt_banks = ctx.enter_context(tc.psum_pool(name="xt_banks", bufs=2))
        at_banks = ctx.enter_context(tc.psum_pool(name="at_banks", bufs=1))
        lora_banks = ctx.enter_context(tc.psum_pool(name="lora_banks", bufs=2))
        base_banks = ctx.enter_context(tc.psum_pool(name="base_banks", bufs=3))
        ctx.enter_context(tc.manual_schedule())

        def pieces(pair):
            return BLOCKS // GROUP if pair == 0 else 1

        def row_tiles(name, width):
            return [
                [
                    keep.tile([P, PAIR * (BLOCKS // pieces(pair)) * width], BF16, name="%s%d%d" % (name, pair, piece))
                    for piece in range(pieces(pair))
                ]
                for pair in range(PAIRS)
            ]

        x_sb = row_tiles("x_sb", MUL)
        a_sb = row_tiles("a_sb", RANK)
        w_raw = [keep.tile([P, PACK * MUL], BF16, name="w_raw%d" % k) for k in range(IRREPS)]
        w_codes = [keep.tile([P, MUL], U32, name="w_codes%d" % k, align_bytes=64) for k in range(IRREPS)]
        w_scales = [keep.tile([P, MUL], U8, name="w_scales%d" % k, align_bytes=64) for k in range(IRREPS)]
        wb_sb = [keep.tile([P, MUL], BF16, name="wb_sb%d" % k) for k in range(IRREPS)]
        ident_f32 = keep.tile([P, P], F32, name="ident_f32")
        ident_bf16 = keep.tile([P, P], BF16, name="ident_bf16")

        def place(step):
            pair, position = divmod(step, BLOCKS)
            return pair, BLOCKS - 1 - position

        def load_rows(pair, piece):
            rows = slice(PAIR * pair, PAIR * (pair + 1))
            blocks = BLOCKS // pieces(pair)
            for sb, dram, width in ((x_sb, x_rows, MUL), (a_sb, a_rows, RANK)):
                cols = slice(piece * blocks * width, (piece + 1) * blocks * width)
                nc.sync.dma_start(
                    out=sb[pair][piece][:].rearrange("p (i c) -> p i c", i=PAIR), in_=dram[:, rows, cols]
                )

        def block_of(sb, pair, i, j, width):
            blocks = BLOCKS // pieces(pair)
            return sb[pair][j // blocks], (i * blocks + j % blocks) * width

        def load_weights(k):
            nc.sync.dma_start(
                out=w_raw[k][:].rearrange("q (u ec) -> q u ec", u=HALVES),
                in_=w_base[k, :, :].rearrange("(u q e) c -> q u (e c)", u=HALVES, e=2),
            )
            nc.sync.dma_start(out=wb_sb[k][:], in_=w_lora_b[k, :, :])

        def quantise_weights(k):
            w_grouped = w_work.tile([P, MUL, PACK], BF16, name="w_grouped", align_bytes=64)
            nc.vector.tensor_copy(
                out=w_grouped[:].rearrange("q (c r) t -> q c t r", r=4),
                in_=w_raw[k][:].rearrange("q (t c r) -> q c t r", t=PACK, r=4),
            )
            nc.vector.quantize_mx(
                out=w_codes[k][:].bitcast(FP8X4),
                scales=w_scales[k][:],
                in_=w_grouped[:].rearrange("q c t -> q (c t)"),
            )

        def transpose_row_tile(step, i, xt, at):
            pair, j = place(step)
            x_tile, first = block_of(x_sb, pair, i, j, MUL)
            for u in range(HALVES):
                word = first // 2 + u * P
                nc.tensor.transpose(xt[:, i, u, :], x_tile[:].bitcast(F32)[:, word : word + P], ident_f32[:])
            if step % GROUP == 0:
                for later in range(GROUP):
                    a_tile, first = block_of(a_sb, pair, i, j - later, RANK)
                    nc.tensor.transpose(at[:, later, i, :], a_tile[:, first : first + RANK], ident_bf16[:])

        load_weights(2)
        load_rows(0, 2)
        load_weights(1)
        load_rows(0, 1)
        load_weights(0)
        load_rows(0, 0)
        for pair in range(1, PAIRS):
            load_rows(pair, 0)

        make_identity(nc, ident_f32[:])
        make_identity(nc, ident_bf16[:])

        a_t = {}
        x_codes = {}
        x_scales = {}
        stage = None

        at = None
        for step in range(-WEIGHT_LEAD, STEPS):
            ahead = step + LOOKAHEAD
            multiply = step >= 0
            prepare = 0 <= ahead < STEPS
            new_group = prepare and ahead % GROUP == 0
            if multiply:
                pair, j = place(step)
                k = IRREP_OF_BLOCK[j]
                together = 1 if step >= STEPS - GROUP else GROUP
                if j % together == together - 1:
                    stage = stages.tile([P, PAIR, together * MUL], F32, name="stage")
                cols = slice((j % together) * MUL, (j % together + 1) * MUL)
            if prepare:
                xt = xt_banks.tile([P, PAIR, HALVES, P], F32, name="xt")
            if new_group:
                at = at_banks.tile([P, GROUP, PAIR, P], BF16, name="at")

            lora = []
            for i in range(PAIR):
                if multiply:
                    lora_ps = lora_banks.tile([P, MUL], F32, name="lora_ps")
                    nc.tensor.matmul(
                        lora_ps[:],
                        lhsT=a_t[step // GROUP][:, step % GROUP, i, :],
                        rhs=wb_sb[k][:],
                        start=True,
                        stop=True,
                    )
                    lora.append(lora_ps)
                if prepare:
                    transpose_row_tile(ahead, i, xt, at)

            if multiply:
                for i in range(PAIR):
                    nc.scalar.mul(out=stage[:, i, cols], in_=lora[i][:], mul=LORA_FACTOR)
            if prepare:
                x_grouped = x_work.tile([P, PAIR * P * PACK], BF16, name="x_grouped", align_bytes=64)
                nc.scalar.copy(
                    out=x_grouped[:].bitcast(F32).rearrange("q (i n u) -> q i n u", i=PAIR, u=HALVES),
                    in_=xt[:].rearrange("q i u n -> q i n u"),
                )

            base = []
            if multiply:
                for i in range(PAIR):
                    nodes = slice(i * P, (i + 1) * P)
                    base_ps = base_banks.tile([P, MUL], F32, name="base_ps")
                    nc.tensor.matmul_mx(
                        out=base_ps[:],
                        lhsT=x_codes[step][:, nodes].bitcast(FP8X4),
                        lhsT_scale=x_scales[step][:, nodes],
                        rhs=w_codes[k][:].bitcast(FP8X4),
                        rhs_scale=w_scales[k][:],
                        start=True,
                        stop=True,
                    )
                    base.append(base_ps)

            def finish(i):
                nc.vector.scalar_tensor_tensor(
                    out=stage[:, i, cols], in0=base[i][:], scalar=BASE_FACTOR, in1=stage[:, i, cols],
                    op0=MULT, op1=ADD,
                )

            if step + WEIGHT_LEAD in FIRST_USE:
                quantise_weights(FIRST_USE[step + WEIGHT_LEAD])
            if multiply:
                finish(0)
            if new_group:
                a_t[ahead // GROUP] = a_ready.tile([P, GROUP, PAIR, P], BF16, name="a_t")
                nc.vector.tensor_copy(out=a_t[ahead // GROUP][:], in_=at[:])
            if multiply:
                finish(1)
            if prepare:
                x_codes[ahead] = ready.tile([P, PAIR * P], U32, name="x_codes", align_bytes=64)
                x_scales[ahead] = ready.tile([P, PAIR * P], U8, name="x_scales", align_bytes=64)
                nc.vector.quantize_mx(
                    out=x_codes[ahead][:].bitcast(FP8X4), scales=x_scales[ahead][:], in_=x_grouped[:]
                )

            if multiply and j % together == 0:
                nc.sync.dma_start(
                    out=out_rows[:, PAIR * pair : PAIR * (pair + 1), j * MUL : (j + together) * MUL], in_=stage[:]
                )
